import numpy as np
import ml_dtypes


def mxq(x, axis, fmt="e4m3"):
    dtype, down = {"e4m3": (ml_dtypes.float8_e4m3fn, 7), "e5m2": (ml_dtypes.float8_e5m2, 14)}[fmt]
    v = np.moveaxis(np.asarray(x, np.float32).astype(ml_dtypes.bfloat16).astype(np.float64), axis, -1)
    blocks = v.reshape(v.shape[:-1] + (-1, 32))
    amax = np.abs(blocks).max(-1, keepdims=True)
    byte = np.maximum(np.where(amax > 0, np.frexp(amax)[1] - 1 + 127, 0) - down, 1)
    scale = np.exp2(byte - 127.0)
    codes = (blocks / scale).astype(np.float32).astype(dtype).astype(np.float64)
    return np.moveaxis((codes * scale).reshape(v.shape), -1, axis)


WIDE = False


def mx_kscale(k):
    if not WIDE:
        return np.ones(k)
    levels = np.array([10, -10, 5, -5, 0])
    a = np.random.permutation(np.resize(levels, k // 512 * 4)).reshape(k // 512, 4)
    idx = np.arange(k)
    return np.exp2(a[idx // 512, idx % 128 // 32])


BF16 = ml_dtypes.bfloat16


def bf(x):
    return np.asarray(x, np.float32).astype(BF16)


def f64(x):
    return np.asarray(x).astype(np.float64)


B, S, D, F, F2 = 2, 128, 256, 1024, 512
EPS = 1e-6
D2 = 2 * D


def setup_inputs():
    n = np.random.standard_normal
    s, t = mx_kscale(F), mx_kscale(D2)
    tr, ti = t[:D], t[D:]
    wd = 1.5 / np.sqrt(F)
    return {'h_r': bf(n((B, S, F)) * 0.6 * s), 'h_i': bf(n((B, S, F)) * 0.6 * s),
            'w2r': bf(n((F, D)) * wd / s[:, None] * tr), 'b2r': bf(n(D) * 0.2 * tr),
            'w2i': bf(n((F, D)) * wd / s[:, None] * ti), 'b2i': bf(n(D) * 0.2 * ti),
            'We': bf(n((D2, D)) / np.sqrt(D2) / t[:, None]), 'be': bf(n(D) * 0.2),
            'g_rms': bf(1.0 + 0.1 * n(D))}


def reference(h_r, h_i, w2r, b2r, w2i, b2i, We, be, g_rms):
    rp = (mxq(f64(h_r), 2, 'e4m3') @ mxq(f64(w2r), 0, 'e4m3')) + f64(b2r)
    ip = (mxq(f64(h_i), 2, 'e4m3') @ mxq(f64(w2i), 0, 'e4m3')) + f64(b2i)
    cat = np.concatenate([rp, ip], axis=-1)
    wave = (mxq(cat, 2, 'e4m3') @ mxq(f64(We), 0, 'e4m3')) + f64(be)
    return wave * (1.0 / np.sqrt(np.mean(wave * wave, axis=-1, keepdims=True) + EPS)) * f64(g_rms)

@@ -1,0 +1,199 @@
+from contextlib import ExitStack
+
+import concourse.mybir as mybir
+from concourse.masks import make_identity
+
+F32 = mybir.dt.float32
+BF16 = mybir.dt.bfloat16
+U32 = mybir.dt.uint32
+U8 = mybir.dt.uint8
+FP8X4 = mybir.dt.float8_e4m3fn_x4
+ADD = mybir.AluOpType.add
+MULT = mybir.AluOpType.mult
+ACT = mybir.ActivationFunctionType
+
+P = 128
+PACK = 4
+K_PASS = P * PACK
+TOKENS = 256
+HID = 1024
+D = 256
+D2 = 2 * D
+EPS = 1e-6
+STREAMS = 2
+HALVES = TOKENS // P
+PASSES = HID // K_PASS
+CHUNKS = D2 // P
+CHUNKS_PER_STREAM = D // P
+RUN = 4
+VECTOR_COLS = 128
+
+FLOPS = 2 * TOKENS * HID * D * STREAMS + 2 * TOKENS * D2 * D
+
+
+def tile_wavenetworklm_pb_s_kernel(tc, h_r, h_i, w2r, b2r, w2i, b2i, We, be, g_rms, out):
+    nc = tc.nc
+    hidden = (h_r, h_i)
+    weights = (w2r, w2i)
+    biases = (b2r, b2i)
+
+    with ExitStack() as ctx:
+        keep = ctx.enter_context(tc.tile_pool(name="keep", bufs=1))
+        psum_xt = ctx.enter_context(tc.psum_pool(name="psum_xt", bufs=STREAMS * HALVES))
+        psum_cat = ctx.enter_context(tc.psum_pool(name="psum_cat", bufs=1))
+        psum_misc = ctx.enter_context(tc.psum_pool(name="psum_misc", bufs=2))
+
+        b2_rows = keep.tile([P, P], BF16)
+        nc.vector.memset(b2_rows[:], 0.0)
+        free_rows = keep.tile([P, 2 * D], BF16)
+        nc.vector.memset(free_rows[:], 0.0)
+        ones = keep.tile([P, P], BF16)
+        nc.vector.memset(ones[:], 1.0)
+        ident_f32 = keep.tile([P, P], F32)
+        make_identity(nc, ident_f32[:])
+        ident_bf16 = keep.tile([P, P], BF16)
+        make_identity(nc, ident_bf16[:])
+
+        for s in range(STREAMS):
+            nc.scalar.dma_start(
+                out=b2_rows[CHUNKS_PER_STREAM * s : CHUNKS_PER_STREAM * (s + 1), :],
+                in_=biases[s].rearrange("(c p) -> c p", p=P),
+            )
+        nc.scalar.dma_start(out=free_rows[0:1, 0:D], in_=be.rearrange("(o n) -> o n", o=1))
+        nc.scalar.dma_start(out=free_rows[0:1, D : 2 * D], in_=g_rms.rearrange("(o n) -> o n", o=1))
+
+        sqrt_in = keep.tile([P, 1], F32)
+        sqrt_out = keep.tile([P, 1], F32)
+        nc.vector.memset(sqrt_in[:], 1.0)
+        nc.scalar.activation(out=sqrt_out[:], in_=sqrt_in[:], func=ACT.Sqrt)
+
+        x_sb = {}
+        w_raw = {}
+        for s in range(STREAMS):
+            tokens = hidden[s].flatten_outer_dims().rearrange("(p j) k -> p j k", j=HALVES)
+            rows = weights[s].rearrange("(g u p e) c -> g p u e c", g=PASSES, u=2, p=P, e=2)
+            w_raw[s] = keep.tile([P, PASSES, PACK, D], BF16, name="w_raw%d" % s)
+            for half in range(HALVES):
+                x_sb[s, half] = keep.tile([P, HID], BF16, name="x_sb%d%d" % (s, half))
+                nc.sync.dma_start(out=x_sb[s, half][:], in_=tokens[:, half, :])
+                nc.sync.dma_start(
+                    out=w_raw[s][:, half, :, :].rearrange("p (u e) c -> p u e c", u=2),
+                    in_=rows[half],
+                )
+        we_raw = keep.tile([P, PACK, D], BF16)
+        nc.sync.dma_start(out=we_raw[:], in_=We.rearrange("(t p) n -> p t n", p=P))
+
+        b2_ps = psum_misc.tile([P, P], BF16, tag="misc")
+        nc.tensor.transpose(b2_ps[:], b2_rows[:], ident_bf16[:])
+        b2_cols = keep.tile([P, CHUNKS], F32)
+        nc.vector.tensor_copy(out=b2_cols[:], in_=b2_ps[:, 0:CHUNKS])
+        spread_ps = psum_misc.tile([P, 2 * D], F32, tag="misc")
+        nc.tensor.matmul(out=spread_ps[:], lhsT=ones[:], rhs=free_rows[:], start=True, stop=True)
+        spread = keep.tile([P, 2 * D], F32)
+        nc.scalar.copy(out=spread[:], in_=spread_ps[:])
+        be_all = spread[:, 0:D]
+        g_all = spread[:, D : 2 * D]
+
+        def interleave_rows(raw, grouped):
+            vector_cols = slice(0, VECTOR_COLS)
+            scalar_cols = slice(VECTOR_COLS, D)
+            nc.vector.tensor_copy(
+                out=grouped[:, vector_cols, :].rearrange("p (c i) t -> p c t i", i=RUN),
+                in_=raw[:, :, vector_cols].rearrange("p t (c i) -> p c t i", i=RUN),
+            )
+            nc.scalar.copy(
+                out=grouped[:, scalar_cols, :].rearrange("p (c i) t -> p c t i", i=RUN),
+                in_=raw[:, :, scalar_cols].rearrange("p t (c i) -> p c t i", i=RUN),
+            )
+
+        def quantise(grouped_flat, codes, scales):
+            nc.vector.quantize_mx(out=codes.bitcast(FP8X4), scales=scales, in_=grouped_flat)
+
+        cat_ps = [
+            psum_cat.tile([P, CHUNKS, P], F32, name="cat_ps%d" % j) for j in range(HALVES)
+        ]
+        for s in range(STREAMS):
+            h_codes = keep.tile([P, HALVES, PASSES, P], U32, name="h_codes%d" % s, align_bytes=64)
+            h_scales = keep.tile([P, HALVES, PASSES, P], U8, name="h_scales%d" % s, align_bytes=64)
+            w_codes = keep.tile([P, PASSES, D], U32, name="w_codes%d" % s, align_bytes=64)
+            w_scales = keep.tile([P, PASSES, D], U8, name="w_scales%d" % s, align_bytes=64)
+            for half in range(HALVES):
+                words = x_sb[s, half][:].bitcast(F32)
+                xt = psum_xt.tile([P, PASSES * 2, P], F32, tag="xt")
+                for q in range(PASSES * 2):
+                    nc.tensor.transpose(xt[:, q, :], words[:, P * q : P * (q + 1)], ident_f32[:])
+                h_grp = keep.tile([P, PASSES, P, PACK], BF16, name="h_grp%d%d" % (s, half), align_bytes=64)
+                nc.scalar.copy(
+                    out=h_grp[:].bitcast(F32),
+                    in_=xt[:].rearrange("p (g u) r -> p g r u", u=2),
+                )
+                w_grp = keep.tile([P, D, PACK], BF16, name="w_grp%d%d" % (s, half), align_bytes=64)
+                interleave_rows(w_raw[s][:, half, :, :], w_grp)
+                quantise(
+                    h_grp[:].rearrange("p g r t -> p (g r t)"),
+                    h_codes[:, half, :, :].rearrange("p g r -> p (g r)"),
+                    h_scales[:, half, :, :].rearrange("p g r -> p (g r)"),
+                )
+                quantise(
+                    w_grp[:].rearrange("p c t -> p (c t)"),
+                    w_codes[:, half, :],
+                    w_scales[:, half, :],
+                )
+            for j in range(HALVES):
+                for cc in range(CHUNKS_PER_STREAM):
+                    cols = slice(P * cc, P * (cc + 1))
+                    for g in range(PASSES):
+                        nc.tensor.matmul_mx(
+                            out=cat_ps[j][:, CHUNKS_PER_STREAM * s + cc, :],
+                            lhsT=w_codes[:, g, cols].bitcast(FP8X4),
+                            lhsT_scale=w_scales[:, g, cols],
+                            rhs=h_codes[:, j, g, :].bitcast(FP8X4),
+                            rhs_scale=h_scales[:, j, g, :],
+                            start=(g == 0),
+                            stop=(g == PASSES - 1),
+                        )
+
+        we_grp = keep.tile([P, D, PACK], BF16, align_bytes=64)
+        interleave_rows(we_raw[:], we_grp)
+        we_codes = keep.tile([P, D], U32, align_bytes=64)
+        we_scales = keep.tile([P, D], U8, align_bytes=64)
+        quantise(we_grp[:].rearrange("p n t -> p (n t)"), we_codes[:], we_scales[:])
+
+        cat_codes = keep.tile([P, HALVES, P], U32, align_bytes=64)
+        cat_scales = keep.tile([P, HALVES, P], U8, align_bytes=64)
+        out_rows = out.flatten_outer_dims().rearrange("(p j) n -> p j n", j=HALVES)
+        for j in range(HALVES):
+            cat_grp = keep.tile([P, P, CHUNKS], BF16, name="cat_grp%d" % j, align_bytes=64)
+            nc.vector.tensor_tensor(
+                out=cat_grp[:],
+                in0=cat_ps[j][:].rearrange("p c r -> p r c"),
+                in1=b2_cols[:].unsqueeze(1).to_broadcast([P, P, CHUNKS]),
+                op=ADD,
+            )
+            quantise(cat_grp[:].rearrange("p r c -> p (r c)"), cat_codes[:, j, :], cat_scales[:, j, :])
+
+        for j in range(HALVES):
+            wave_ps = psum_misc.tile([P, D], F32, tag="misc")
+            nc.tensor.matmul_mx(
+                out=wave_ps[:],
+                lhsT=cat_codes[:, j, :].bitcast(FP8X4),
+                lhsT_scale=cat_scales[:, j, :],
+                rhs=we_codes[:].bitcast(FP8X4),
+                rhs_scale=we_scales[:],
+                start=True,
+                stop=True,
+            )
+            wave = keep.tile([P, D], F32, name="wave%d" % j)
+            nc.vector.tensor_tensor(out=wave[:], in0=wave_ps[:], in1=be_all, op=ADD)
+            squares = keep.tile([P, D], F32, name="squares%d" % j)
+            sum_sq = keep.tile([P, 1], F32, name="sum_sq%d" % j)
+            nc.scalar.activation(out=squares[:], in_=wave[:], func=ACT.Square, accum_out=sum_sq[:])
+            rms = keep.tile([P, 1], F32, name="rms%d" % j)
+            nc.scalar.activation(out=rms[:], in_=sum_sq[:], func=ACT.Sqrt, scale=1.0 / D, bias=EPS)
+            inv_rms = keep.tile([P, 1], F32, name="inv_rms%d" % j)
+            nc.vector.reciprocal(out=inv_rms[:], in_=rms[:])
+            normed = keep.tile([P, D], F32, name="normed%d" % j)
+            nc.vector.scalar_tensor_tensor(
+                out=normed[:], in0=wave[:], scalar=inv_rms[:, 0:1], in1=g_all, op0=MULT, op1=MULT
+            )
+            nc.sync.dma_start(out=out_rows[:, j, :], in_=normed[:])

@@ -26,7 +26,7 @@ PASSES = HID // K_PASS
 CHUNKS = D2 // P
 CHUNKS_PER_STREAM = D // P
 RUN = 4
-VECTOR_COLS = 128
+VECTOR_COLS = 176
 
 FLOPS = 2 * TOKENS * HID * D * STREAMS + 2 * TOKENS * D2 * D
 
@@ -36,17 +36,52 @@ def tile_wavenetworklm_pb_s_kernel(tc, h_r, h_i, w2r, b2r, w2i, b2i, We, be, g_r
     hidden = (h_r, h_i)
     weights = (w2r, w2i)
     biases = (b2r, b2i)
+    steps = [(s, half) for s in range(STREAMS) for half in range(HALVES)]
 
     with ExitStack() as ctx:
         keep = ctx.enter_context(tc.tile_pool(name="keep", bufs=1))
-        psum_xt = ctx.enter_context(tc.psum_pool(name="psum_xt", bufs=STREAMS * HALVES))
+        psum_xt = ctx.enter_context(tc.psum_pool(name="psum_xt", bufs=len(steps)))
         psum_cat = ctx.enter_context(tc.psum_pool(name="psum_cat", bufs=1))
         psum_misc = ctx.enter_context(tc.psum_pool(name="psum_misc", bufs=2))
+        ctx.enter_context(tc.manual_schedule())
+
+        x_sb = {}
+        w_raw = {}
+        tokens = {}
+        for s in range(STREAMS):
+            x_sb[s] = keep.tile([P, HALVES, HID], BF16, name="x_sb%d" % s)
+            tokens[s] = hidden[s].flatten_outer_dims().rearrange("(p j) k -> p j k", j=HALVES)
+
+        def load_weight_rows(s, g):
+            rows = weights[s].rearrange("(g u p e) c -> g p u e c", g=PASSES, u=2, p=P, e=2)
+            w_raw[s, g] = keep.tile([P, PACK, D], BF16, name="w_raw%d%d" % (s, g))
+            nc.sync.dma_start(out=w_raw[s, g][:].rearrange("p (u e) c -> p u e c", u=2), in_=rows[g])
+
+        for half in range(HALVES):
+            nc.sync.dma_start(out=x_sb[0][:, half, :], in_=tokens[0][:, half, :])
+            load_weight_rows(0, half)
+        nc.sync.dma_start(out=x_sb[1][:], in_=tokens[1])
+        for g in range(PASSES):
+            load_weight_rows(1, g)
+        we_raw = keep.tile([P, PACK, D], BF16)
+        nc.sync.dma_start(out=we_raw[:], in_=We.rearrange("(t p) n -> p t n", p=P))
 
         b2_rows = keep.tile([P, P], BF16)
         nc.vector.memset(b2_rows[:], 0.0)
         free_rows = keep.tile([P, 2 * D], BF16)
         nc.vector.memset(free_rows[:], 0.0)
+        for s in range(STREAMS):
+            nc.sync.dma_start(
+                out=b2_rows[CHUNKS_PER_STREAM * s : CHUNKS_PER_STREAM * (s + 1), :],
+                in_=biases[s].rearrange("(c p) -> c p", p=P),
+            )
+        nc.sync.dma_start(out=free_rows[0:1, 0:D], in_=be.rearrange("(o n) -> o n", o=1))
+        nc.sync.dma_start(out=free_rows[0:1, D : 2 * D], in_=g_rms.rearrange("(o n) -> o n", o=1))
+
+        sqrt_in = keep.tile([P, 1], F32)
+        sqrt_out = keep.tile([P, 1], F32)
+        nc.vector.memset(sqrt_in[:], 1.0)
+        nc.scalar.activation(out=sqrt_out[:], in_=sqrt_in[:], func=ACT.Sqrt)
         ones = keep.tile([P, P], BF16)
         nc.vector.memset(ones[:], 1.0)
         ident_f32 = keep.tile([P, P], F32)
@@ -54,124 +89,100 @@ def tile_wavenetworklm_pb_s_kernel(tc, h_r, h_i, w2r, b2r, w2i, b2i, We, be, g_r
         ident_bf16 = keep.tile([P, P], BF16)
         make_identity(nc, ident_bf16[:])
 
-        for s in range(STREAMS):
-            nc.scalar.dma_start(
-                out=b2_rows[CHUNKS_PER_STREAM * s : CHUNKS_PER_STREAM * (s + 1), :],
-                in_=biases[s].rearrange("(c p) -> c p", p=P),
-            )
-        nc.scalar.dma_start(out=free_rows[0:1, 0:D], in_=be.rearrange("(o n) -> o n", o=1))
-        nc.scalar.dma_start(out=free_rows[0:1, D : 2 * D], in_=g_rms.rearrange("(o n) -> o n", o=1))
-
-        sqrt_in = keep.tile([P, 1], F32)
-        sqrt_out = keep.tile([P, 1], F32)
-        nc.vector.memset(sqrt_in[:], 1.0)
-        nc.scalar.activation(out=sqrt_out[:], in_=sqrt_in[:], func=ACT.Sqrt)
-
-        x_sb = {}
-        w_raw = {}
-        for s in range(STREAMS):
-            tokens = hidden[s].flatten_outer_dims().rearrange("(p j) k -> p j k", j=HALVES)
-            rows = weights[s].rearrange("(g u p e) c -> g p u e c", g=PASSES, u=2, p=P, e=2)
-            w_raw[s] = keep.tile([P, PASSES, PACK, D], BF16, name="w_raw%d" % s)
-            for half in range(HALVES):
-                x_sb[s, half] = keep.tile([P, HID], BF16, name="x_sb%d%d" % (s, half))
-                nc.sync.dma_start(out=x_sb[s, half][:], in_=tokens[:, half, :])
-                nc.sync.dma_start(
-                    out=w_raw[s][:, half, :, :].rearrange("p (u e) c -> p u e c", u=2),
-                    in_=rows[half],
-                )
-        we_raw = keep.tile([P, PACK, D], BF16)
-        nc.sync.dma_start(out=we_raw[:], in_=We.rearrange("(t p) n -> p t n", p=P))
-
+        xt = {}
+        for s, half in steps:
+            words = x_sb[s][:].bitcast(F32)[:, half, :]
+            xt[s, half] = psum_xt.tile([P, PASSES * 2, P], F32, name="xt%d%d" % (s, half), tag="xt")
+            for q in range(PASSES * 2):
+                nc.tensor.transpose(xt[s, half][:, q, :], words[:, P * q : P * (q + 1)], ident_f32[:])
         b2_ps = psum_misc.tile([P, P], BF16, tag="misc")
         nc.tensor.transpose(b2_ps[:], b2_rows[:], ident_bf16[:])
-        b2_cols = keep.tile([P, CHUNKS], F32)
-        nc.vector.tensor_copy(out=b2_cols[:], in_=b2_ps[:, 0:CHUNKS])
         spread_ps = psum_misc.tile([P, 2 * D], F32, tag="misc")
         nc.tensor.matmul(out=spread_ps[:], lhsT=ones[:], rhs=free_rows[:], start=True, stop=True)
-        spread = keep.tile([P, 2 * D], F32)
-        nc.scalar.copy(out=spread[:], in_=spread_ps[:])
-        be_all = spread[:, 0:D]
-        g_all = spread[:, D : 2 * D]
 
-        def interleave_rows(raw, grouped):
-            vector_cols = slice(0, VECTOR_COLS)
-            scalar_cols = slice(VECTOR_COLS, D)
-            nc.vector.tensor_copy(
-                out=grouped[:, vector_cols, :].rearrange("p (c i) t -> p c t i", i=RUN),
-                in_=raw[:, :, vector_cols].rearrange("p t (c i) -> p c t i", i=RUN),
-            )
+        def interleave_rows(raw, grouped, vector_cols):
+            if vector_cols > 0:
+                nc.vector.tensor_copy(
+                    out=grouped[:, 0:vector_cols, :].rearrange("p (c i) t -> p c t i", i=RUN),
+                    in_=raw[:, :, 0:vector_cols].rearrange("p t (c i) -> p c t i", i=RUN),
+                )
             nc.scalar.copy(
-                out=grouped[:, scalar_cols, :].rearrange("p (c i) t -> p c t i", i=RUN),
-                in_=raw[:, :, scalar_cols].rearrange("p t (c i) -> p c t i", i=RUN),
+                out=grouped[:, vector_cols:D, :].rearrange("p (c i) t -> p c t i", i=RUN),
+                in_=raw[:, :, vector_cols:D].rearrange("p t (c i) -> p c t i", i=RUN),
             )
 
         def quantise(grouped_flat, codes, scales):
             nc.vector.quantize_mx(out=codes.bitcast(FP8X4), scales=scales, in_=grouped_flat)
 
+        h_codes = keep.tile([P, STREAMS, HALVES, PASSES, P], U32, align_bytes=64)
+        h_scales = keep.tile([P, STREAMS, HALVES, PASSES, P], U8, align_bytes=64)
+        w_codes = keep.tile([P, STREAMS, PASSES, D], U32, align_bytes=64)
+        w_scales = keep.tile([P, STREAMS, PASSES, D], U8, align_bytes=64)
+        for s, half in steps:
+            h_grp = keep.tile([P, PASSES, P, PACK], BF16, name="h_grp%d%d" % (s, half), align_bytes=64)
+            nc.scalar.copy(
+                out=h_grp[:].bitcast(F32),
+                in_=xt[s, half][:].rearrange("p (g u) r -> p g r u", u=2),
+            )
+            w_grp = keep.tile([P, D, PACK], BF16, name="w_grp%d%d" % (s, half), align_bytes=64)
+            interleave_rows(w_raw[s, half], w_grp, VECTOR_COLS)
+            quantise(
+                h_grp[:].rearrange("p g r t -> p (g r t)"),
+                h_codes[:, s, half, :, :].rearrange("p g r -> p (g r)"),
+                h_scales[:, s, half, :, :].rearrange("p g r -> p (g r)"),
+            )
+            quantise(w_grp[:].rearrange("p c t -> p (c t)"), w_codes[:, s, half, :], w_scales[:, s, half, :])
+
         cat_ps = [
             psum_cat.tile([P, CHUNKS, P], F32, name="cat_ps%d" % j) for j in range(HALVES)
         ]
         for s in range(STREAMS):
-            h_codes = keep.tile([P, HALVES, PASSES, P], U32, name="h_codes%d" % s, align_bytes=64)
-            h_scales = keep.tile([P, HALVES, PASSES, P], U8, name="h_scales%d" % s, align_bytes=64)
-            w_codes = keep.tile([P, PASSES, D], U32, name="w_codes%d" % s, align_bytes=64)
-            w_scales = keep.tile([P, PASSES, D], U8, name="w_scales%d" % s, align_bytes=64)
-            for half in range(HALVES):
-                words = x_sb[s, half][:].bitcast(F32)
-                xt = psum_xt.tile([P, PASSES * 2, P], F32, tag="xt")
-                for q in range(PASSES * 2):
-                    nc.tensor.transpose(xt[:, q, :], words[:, P * q : P * (q + 1)], ident_f32[:])
-                h_grp = keep.tile([P, PASSES, P, PACK], BF16, name="h_grp%d%d" % (s, half), align_bytes=64)
-                nc.scalar.copy(
-                    out=h_grp[:].bitcast(F32),
-                    in_=xt[:].rearrange("p (g u) r -> p g r u", u=2),
-                )
-                w_grp = keep.tile([P, D, PACK], BF16, name="w_grp%d%d" % (s, half), align_bytes=64)
-                interleave_rows(w_raw[s][:, half, :, :], w_grp)
-                quantise(
-                    h_grp[:].rearrange("p g r t -> p (g r t)"),
-                    h_codes[:, half, :, :].rearrange("p g r -> p (g r)"),
-                    h_scales[:, half, :, :].rearrange("p g r -> p (g r)"),
-                )
-                quantise(
-                    w_grp[:].rearrange("p c t -> p (c t)"),
-                    w_codes[:, half, :],
-                    w_scales[:, half, :],
-                )
             for j in range(HALVES):
                 for cc in range(CHUNKS_PER_STREAM):
                     cols = slice(P * cc, P * (cc + 1))
                     for g in range(PASSES):
                         nc.tensor.matmul_mx(
                             out=cat_ps[j][:, CHUNKS_PER_STREAM * s + cc, :],
-                            lhsT=w_codes[:, g, cols].bitcast(FP8X4),
-                            lhsT_scale=w_scales[:, g, cols],
-                            rhs=h_codes[:, j, g, :].bitcast(FP8X4),
-                            rhs_scale=h_scales[:, j, g, :],
+                            lhsT=w_codes[:, s, g, cols].bitcast(FP8X4),
+                            lhsT_scale=w_scales[:, s, g, cols],
+                            rhs=h_codes[:, s, j, g, :].bitcast(FP8X4),
+                            rhs_scale=h_scales[:, s, j, g, :],
                             start=(g == 0),
                             stop=(g == PASSES - 1),
                         )
 
         we_grp = keep.tile([P, D, PACK], BF16, align_bytes=64)
-        interleave_rows(we_raw[:], we_grp)
-        we_codes = keep.tile([P, D], U32, align_bytes=64)
-        we_scales = keep.tile([P, D], U8, align_bytes=64)
-        quantise(we_grp[:].rearrange("p n t -> p (n t)"), we_codes[:], we_scales[:])
+        interleave_rows(we_raw, we_grp, 0)
+        spread = keep.tile([P, 2 * D], F32)
+        nc.scalar.copy(out=spread[:], in_=spread_ps[:])
+        be_all = spread[:, 0:D]
+        g_all = spread[:, D : 2 * D]
 
+        b2_cols = keep.tile([P, CHUNKS], F32)
+        nc.vector.tensor_copy(out=b2_cols[:], in_=b2_ps[:, 0:CHUNKS])
+        cat_grp = keep.tile([P, HALVES, P, CHUNKS], BF16, align_bytes=64)
         cat_codes = keep.tile([P, HALVES, P], U32, align_bytes=64)
         cat_scales = keep.tile([P, HALVES, P], U8, align_bytes=64)
-        out_rows = out.flatten_outer_dims().rearrange("(p j) n -> p j n", j=HALVES)
-        for j in range(HALVES):
-            cat_grp = keep.tile([P, P, CHUNKS], BF16, name="cat_grp%d" % j, align_bytes=64)
+        we_codes = keep.tile([P, D], U32, align_bytes=64)
+        we_scales = keep.tile([P, D], U8, align_bytes=64)
+
+        def add_bias(j):
             nc.vector.tensor_tensor(
-                out=cat_grp[:],
+                out=cat_grp[:, j, :, :],
                 in0=cat_ps[j][:].rearrange("p c r -> p r c"),
                 in1=b2_cols[:].unsqueeze(1).to_broadcast([P, P, CHUNKS]),
                 op=ADD,
             )
-            quantise(cat_grp[:].rearrange("p r c -> p (r c)"), cat_codes[:, j, :], cat_scales[:, j, :])
 
+        add_bias(0)
+        quantise(we_grp[:].rearrange("p n t -> p (n t)"), we_codes[:], we_scales[:])
+        add_bias(1)
+        for j in range(HALVES):
+            quantise(
+                cat_grp[:, j, :, :].rearrange("p r c -> p (r c)"), cat_codes[:, j, :], cat_scales[:, j, :]
+            )
+
+        wave = keep.tile([P, HALVES, D], F32)
         for j in range(HALVES):
             wave_ps = psum_misc.tile([P, D], F32, tag="misc")
             nc.tensor.matmul_mx(
@@ -183,17 +194,19 @@ def tile_wavenetworklm_pb_s_kernel(tc, h_r, h_i, w2r, b2r, w2i, b2i, We, be, g_r
                 start=True,
                 stop=True,
             )
-            wave = keep.tile([P, D], F32, name="wave%d" % j)
-            nc.vector.tensor_tensor(out=wave[:], in0=wave_ps[:], in1=be_all, op=ADD)
+            nc.vector.tensor_tensor(out=wave[:, j, :], in0=wave_ps[:], in1=be_all, op=ADD)
+
+        out_rows = out.flatten_outer_dims().rearrange("(p j) n -> p j n", j=HALVES)
+        for j in range(HALVES):
             squares = keep.tile([P, D], F32, name="squares%d" % j)
             sum_sq = keep.tile([P, 1], F32, name="sum_sq%d" % j)
-            nc.scalar.activation(out=squares[:], in_=wave[:], func=ACT.Square, accum_out=sum_sq[:])
+            nc.scalar.activation(out=squares[:], in_=wave[:, j, :], func=ACT.Square, accum_out=sum_sq[:])
             rms = keep.tile([P, 1], F32, name="rms%d" % j)
             nc.scalar.activation(out=rms[:], in_=sum_sq[:], func=ACT.Sqrt, scale=1.0 / D, bias=EPS)
             inv_rms = keep.tile([P, 1], F32, name="inv_rms%d" % j)
             nc.vector.reciprocal(out=inv_rms[:], in_=rms[:])
             normed = keep.tile([P, D], F32, name="normed%d" % j)
             nc.vector.scalar_tensor_tensor(
-                out=normed[:], in0=wave[:], scalar=inv_rms[:, 0:1], in1=g_all, op0=MULT, op1=MULT
+                out=normed[:], in0=wave[:, j, :], scalar=inv_rms[:, 0:1], in1=g_all, op0=MULT, op1=MULT
             )
             nc.sync.dma_start(out=out_rows[:, j, :], in_=normed[:])

@@ -26,7 +26,6 @@ PASSES = HID // K_PASS
 CHUNKS = D2 // P
 CHUNKS_PER_STREAM = D // P
 RUN = 4
-VECTOR_COLS = 176
 
 FLOPS = 2 * TOKENS * HID * D * STREAMS + 2 * TOKENS * D2 * D
 
@@ -36,33 +35,34 @@ def tile_wavenetworklm_pb_s_kernel(tc, h_r, h_i, w2r, b2r, w2i, b2i, We, be, g_r
     hidden = (h_r, h_i)
     weights = (w2r, w2i)
     biases = (b2r, b2i)
-    steps = [(s, half) for s in range(STREAMS) for half in range(HALVES)]
+    units = [(s, j) for j in range(HALVES) for s in range(STREAMS)]
 
     with ExitStack() as ctx:
         keep = ctx.enter_context(tc.tile_pool(name="keep", bufs=1))
-        psum_xt = ctx.enter_context(tc.psum_pool(name="psum_xt", bufs=len(steps)))
+        psum_xt = ctx.enter_context(tc.psum_pool(name="psum_xt", bufs=len(units)))
         psum_cat = ctx.enter_context(tc.psum_pool(name="psum_cat", bufs=1))
         psum_misc = ctx.enter_context(tc.psum_pool(name="psum_misc", bufs=2))
         ctx.enter_context(tc.manual_schedule())
 
         x_sb = {}
         w_raw = {}
-        tokens = {}
-        for s in range(STREAMS):
-            x_sb[s] = keep.tile([P, HALVES, HID], BF16, name="x_sb%d" % s)
-            tokens[s] = hidden[s].flatten_outer_dims().rearrange("(p j) k -> p j k", j=HALVES)
+
+        def load_tokens(s, j):
+            tokens = hidden[s].flatten_outer_dims().rearrange("(p j) k -> p j k", j=HALVES)
+            x_sb[s, j] = keep.tile([P, HID], BF16, name="x_sb%d%d" % (s, j))
+            nc.sync.dma_start(out=x_sb[s, j][:], in_=tokens[:, j, :])
 
         def load_weight_rows(s, g):
             rows = weights[s].rearrange("(g u p e) c -> g p u e c", g=PASSES, u=2, p=P, e=2)
             w_raw[s, g] = keep.tile([P, PACK, D], BF16, name="w_raw%d%d" % (s, g))
             nc.sync.dma_start(out=w_raw[s, g][:].rearrange("p (u e) c -> p u e c", u=2), in_=rows[g])
 
-        for half in range(HALVES):
-            nc.sync.dma_start(out=x_sb[0][:, half, :], in_=tokens[0][:, half, :])
-            load_weight_rows(0, half)
-        nc.sync.dma_start(out=x_sb[1][:], in_=tokens[1])
-        for g in range(PASSES):
-            load_weight_rows(1, g)
+        for s in range(STREAMS):
+            load_tokens(s, 0)
+            for g in range(PASSES):
+                load_weight_rows(s, g)
+        for s in range(STREAMS):
+            load_tokens(s, 1)
         we_raw = keep.tile([P, PACK, D], BF16)
         nc.sync.dma_start(out=we_raw[:], in_=We.rearrange("(t p) n -> p t n", p=P))
 
@@ -90,69 +90,70 @@ def tile_wavenetworklm_pb_s_kernel(tc, h_r, h_i, w2r, b2r, w2i, b2i, We, be, g_r
         make_identity(nc, ident_bf16[:])
 
         xt = {}
-        for s, half in steps:
-            words = x_sb[s][:].bitcast(F32)[:, half, :]
-            xt[s, half] = psum_xt.tile([P, PASSES * 2, P], F32, name="xt%d%d" % (s, half), tag="xt")
+        for s, j in units:
+            words = x_sb[s, j][:].bitcast(F32)
+            xt[s, j] = psum_xt.tile([P, PASSES * 2, P], F32, name="xt%d%d" % (s, j), tag="xt")
             for q in range(PASSES * 2):
-                nc.tensor.transpose(xt[s, half][:, q, :], words[:, P * q : P * (q + 1)], ident_f32[:])
+                nc.tensor.transpose(xt[s, j][:, q, :], words[:, P * q : P * (q + 1)], ident_f32[:])
         b2_ps = psum_misc.tile([P, P], BF16, tag="misc")
         nc.tensor.transpose(b2_ps[:], b2_rows[:], ident_bf16[:])
-        spread_ps = psum_misc.tile([P, 2 * D], F32, tag="misc")
-        nc.tensor.matmul(out=spread_ps[:], lhsT=ones[:], rhs=free_rows[:], start=True, stop=True)
 
-        def interleave_rows(raw, grouped, vector_cols):
-            if vector_cols > 0:
-                nc.vector.tensor_copy(
-                    out=grouped[:, 0:vector_cols, :].rearrange("p (c i) t -> p c t i", i=RUN),
-                    in_=raw[:, :, 0:vector_cols].rearrange("p t (c i) -> p c t i", i=RUN),
-                )
-            nc.scalar.copy(
-                out=grouped[:, vector_cols:D, :].rearrange("p (c i) t -> p c t i", i=RUN),
-                in_=raw[:, :, vector_cols:D].rearrange("p t (c i) -> p c t i", i=RUN),
+        def interleaved(grouped, raw):
+            return dict(
+                out=grouped[:].rearrange("p (c i) t -> p c t i", i=RUN),
+                in_=raw[:].rearrange("p t (c i) -> p c t i", i=RUN),
             )
 
         def quantise(grouped_flat, codes, scales):
             nc.vector.quantize_mx(out=codes.bitcast(FP8X4), scales=scales, in_=grouped_flat)
 
-        h_codes = keep.tile([P, STREAMS, HALVES, PASSES, P], U32, align_bytes=64)
-        h_scales = keep.tile([P, STREAMS, HALVES, PASSES, P], U8, align_bytes=64)
+        h_grp = {}
+        for s, j in units:
+            h_grp[s, j] = keep.tile([P, PASSES, P, PACK], BF16, name="h_grp%d%d" % (s, j), align_bytes=64)
+            nc.scalar.copy(
+                out=h_grp[s, j][:].bitcast(F32),
+                in_=xt[s, j][:].rearrange("p (g u) r -> p g r u", u=2),
+            )
+        we_grp = keep.tile([P, D, PACK], BF16, align_bytes=64)
+        nc.scalar.copy(**interleaved(we_grp, we_raw))
+
         w_codes = keep.tile([P, STREAMS, PASSES, D], U32, align_bytes=64)
         w_scales = keep.tile([P, STREAMS, PASSES, D], U8, align_bytes=64)
-        for s, half in steps:
-            h_grp = keep.tile([P, PASSES, P, PACK], BF16, name="h_grp%d%d" % (s, half), align_bytes=64)
-            nc.scalar.copy(
-                out=h_grp[:].bitcast(F32),
-                in_=xt[s, half][:].rearrange("p (g u) r -> p g r u", u=2),
-            )
-            w_grp = keep.tile([P, D, PACK], BF16, name="w_grp%d%d" % (s, half), align_bytes=64)
-            interleave_rows(w_raw[s, half], w_grp, VECTOR_COLS)
+        for s in range(STREAMS):
+            w_grp = {}
+            for g in range(PASSES):
+                w_grp[g] = keep.tile([P, D, PACK], BF16, name="w_grp%d%d" % (s, g), align_bytes=64)
+                nc.vector.tensor_copy(**interleaved(w_grp[g], w_raw[s, g]))
+            for g in range(PASSES):
+                quantise(w_grp[g][:].rearrange("p c t -> p (c t)"), w_codes[:, s, g, :], w_scales[:, s, g, :])
+        h_codes = keep.tile([P, STREAMS, HALVES, PASSES, P], U32, align_bytes=64)
+        h_scales = keep.tile([P, STREAMS, HALVES, PASSES, P], U8, align_bytes=64)
+        for s, j in units:
             quantise(
-                h_grp[:].rearrange("p g r t -> p (g r t)"),
-                h_codes[:, s, half, :, :].rearrange("p g r -> p (g r)"),
-                h_scales[:, s, half, :, :].rearrange("p g r -> p (g r)"),
+                h_grp[s, j][:].rearrange("p g r t -> p (g r t)"),
+                h_codes[:, s, j, :, :].rearrange("p g r -> p (g r)"),
+                h_scales[:, s, j, :, :].rearrange("p g r -> p (g r)"),
             )
-            quantise(w_grp[:].rearrange("p c t -> p (c t)"), w_codes[:, s, half, :], w_scales[:, s, half, :])
 
         cat_ps = [
             psum_cat.tile([P, CHUNKS, P], F32, name="cat_ps%d" % j) for j in range(HALVES)
         ]
-        for s in range(STREAMS):
-            for j in range(HALVES):
-                for cc in range(CHUNKS_PER_STREAM):
-                    cols = slice(P * cc, P * (cc + 1))
-                    for g in range(PASSES):
-                        nc.tensor.matmul_mx(
-                            out=cat_ps[j][:, CHUNKS_PER_STREAM * s + cc, :],
-                            lhsT=w_codes[:, s, g, cols].bitcast(FP8X4),
-                            lhsT_scale=w_scales[:, s, g, cols],
-                            rhs=h_codes[:, s, j, g, :].bitcast(FP8X4),
-                            rhs_scale=h_scales[:, s, j, g, :],
-                            start=(g == 0),
-                            stop=(g == PASSES - 1),
-                        )
+        for s, j in units:
+            for cc in range(CHUNKS_PER_STREAM):
+                cols = slice(P * cc, P * (cc + 1))
+                for g in range(PASSES):
+                    nc.tensor.matmul_mx(
+                        out=cat_ps[j][:, CHUNKS_PER_STREAM * s + cc, :],
+                        lhsT=w_codes[:, s, g, cols].bitcast(FP8X4),
+                        lhsT_scale=w_scales[:, s, g, cols],
+                        rhs=h_codes[:, s, j, g, :].bitcast(FP8X4),
+                        rhs_scale=h_scales[:, s, j, g, :],
+                        start=(g == 0),
+                        stop=(g == PASSES - 1),
+                    )
 
-        we_grp = keep.tile([P, D, PACK], BF16, align_bytes=64)
-        interleave_rows(we_raw, we_grp, 0)
+        spread_ps = psum_misc.tile([P, 2 * D], F32, tag="misc")
+        nc.tensor.matmul(out=spread_ps[:], lhsT=ones[:], rhs=free_rows[:], start=True, stop=True)
         spread = keep.tile([P, 2 * D], F32)
         nc.scalar.copy(out=spread[:], in_=spread_ps[:])
         be_all = spread[:, 0:D]
@@ -165,8 +166,12 @@ def tile_wavenetworklm_pb_s_kernel(tc, h_r, h_i, w2r, b2r, w2i, b2i, We, be, g_r
         cat_scales = keep.tile([P, HALVES, P], U8, align_bytes=64)
         we_codes = keep.tile([P, D], U32, align_bytes=64)
         we_scales = keep.tile([P, D], U8, align_bytes=64)
+        wave = keep.tile([P, HALVES, D], F32)
+        wave_ps = {}
+        rms = {}
+        out_rows = out.flatten_outer_dims().rearrange("(p j) n -> p j n", j=HALVES)
 
-        def add_bias(j):
+        def add_b2(j):
             nc.vector.tensor_tensor(
                 out=cat_grp[:, j, :, :],
                 in0=cat_ps[j][:].rearrange("p c r -> p r c"),
@@ -174,19 +179,13 @@ def tile_wavenetworklm_pb_s_kernel(tc, h_r, h_i, w2r, b2r, w2i, b2i, We, be, g_r
                 op=ADD,
             )
 
-        add_bias(0)
-        quantise(we_grp[:].rearrange("p n t -> p (n t)"), we_codes[:], we_scales[:])
-        add_bias(1)
-        for j in range(HALVES):
+        def second_contraction(j):
             quantise(
                 cat_grp[:, j, :, :].rearrange("p r c -> p (r c)"), cat_codes[:, j, :], cat_scales[:, j, :]
             )
-
-        wave = keep.tile([P, HALVES, D], F32)
-        for j in range(HALVES):
-            wave_ps = psum_misc.tile([P, D], F32, tag="misc")
+            wave_ps[j] = psum_misc.tile([P, D], F32, name="wave_ps%d" % j, tag="misc")
             nc.tensor.matmul_mx(
-                out=wave_ps[:],
+                out=wave_ps[j][:],
                 lhsT=cat_codes[:, j, :].bitcast(FP8X4),
                 lhsT_scale=cat_scales[:, j, :],
                 rhs=we_codes[:].bitcast(FP8X4),
@@ -194,19 +193,30 @@ def tile_wavenetworklm_pb_s_kernel(tc, h_r, h_i, w2r, b2r, w2i, b2i, We, be, g_r
                 start=True,
                 stop=True,
             )
-            nc.vector.tensor_tensor(out=wave[:, j, :], in0=wave_ps[:], in1=be_all, op=ADD)
 
-        out_rows = out.flatten_outer_dims().rearrange("(p j) n -> p j n", j=HALVES)
-        for j in range(HALVES):
+        def add_be_and_measure(j):
+            nc.vector.tensor_tensor(out=wave[:, j, :], in0=wave_ps[j][:], in1=be_all, op=ADD)
             squares = keep.tile([P, D], F32, name="squares%d" % j)
             sum_sq = keep.tile([P, 1], F32, name="sum_sq%d" % j)
             nc.scalar.activation(out=squares[:], in_=wave[:, j, :], func=ACT.Square, accum_out=sum_sq[:])
-            rms = keep.tile([P, 1], F32, name="rms%d" % j)
-            nc.scalar.activation(out=rms[:], in_=sum_sq[:], func=ACT.Sqrt, scale=1.0 / D, bias=EPS)
+            rms[j] = keep.tile([P, 1], F32, name="rms%d" % j)
+            nc.scalar.activation(out=rms[j][:], in_=sum_sq[:], func=ACT.Sqrt, scale=1.0 / D, bias=EPS)
+
+        def normalise_and_store(j):
             inv_rms = keep.tile([P, 1], F32, name="inv_rms%d" % j)
-            nc.vector.reciprocal(out=inv_rms[:], in_=rms[:])
+            nc.vector.reciprocal(out=inv_rms[:], in_=rms[j][:])
             normed = keep.tile([P, D], F32, name="normed%d" % j)
             nc.vector.scalar_tensor_tensor(
                 out=normed[:], in0=wave[:, j, :], scalar=inv_rms[:, 0:1], in1=g_all, op0=MULT, op1=MULT
             )
             nc.sync.dma_start(out=out_rows[:, j, :], in_=normed[:])
+
+        add_b2(0)
+        quantise(we_grp[:].rearrange("p n t -> p (n t)"), we_codes[:], we_scales[:])
+        second_contraction(0)
+        add_b2(1)
+        add_be_and_measure(0)
+        second_contraction(1)
+        add_be_and_measure(1)
+        normalise_and_store(0)
+        normalise_and_store(1)

@@ -26,6 +26,7 @@ PASSES = HID // K_PASS
 CHUNKS = D2 // P
 CHUNKS_PER_STREAM = D // P
 RUN = 4
+VECTOR_COLS = 176
 
 FLOPS = 2 * TOKENS * HID * D * STREAMS + 2 * TOKENS * D2 * D
 
@@ -36,6 +37,7 @@ def tile_wavenetworklm_pb_s_kernel(tc, h_r, h_i, w2r, b2r, w2i, b2i, We, be, g_r
     weights = (w2r, w2i)
     biases = (b2r, b2i)
     units = [(s, j) for j in range(HALVES) for s in range(STREAMS)]
+    pieces = [(s, g) for s in range(STREAMS) for g in range(PASSES)]
 
     with ExitStack() as ctx:
         keep = ctx.enter_context(tc.tile_pool(name="keep", bufs=1))
@@ -46,23 +48,13 @@ def tile_wavenetworklm_pb_s_kernel(tc, h_r, h_i, w2r, b2r, w2i, b2i, We, be, g_r
 
         x_sb = {}
         w_raw = {}
-
-        def load_tokens(s, j):
+        for (s, j), (ws, g) in zip(units, pieces):
             tokens = hidden[s].flatten_outer_dims().rearrange("(p j) k -> p j k", j=HALVES)
             x_sb[s, j] = keep.tile([P, HID], BF16, name="x_sb%d%d" % (s, j))
             nc.sync.dma_start(out=x_sb[s, j][:], in_=tokens[:, j, :])
-
-        def load_weight_rows(s, g):
-            rows = weights[s].rearrange("(g u p e) c -> g p u e c", g=PASSES, u=2, p=P, e=2)
-            w_raw[s, g] = keep.tile([P, PACK, D], BF16, name="w_raw%d%d" % (s, g))
-            nc.sync.dma_start(out=w_raw[s, g][:].rearrange("p (u e) c -> p u e c", u=2), in_=rows[g])
-
-        for s in range(STREAMS):
-            load_tokens(s, 0)
-            for g in range(PASSES):
-                load_weight_rows(s, g)
-        for s in range(STREAMS):
-            load_tokens(s, 1)
+            rows = weights[ws].rearrange("(g p t) c -> g p t c", g=PASSES, p=P, t=PACK)
+            w_raw[ws, g] = keep.tile([P, PACK, D], BF16, name="w_raw%d%d" % (ws, g))
+            nc.sync.dma_start(out=w_raw[ws, g][:], in_=rows[g])
         we_raw = keep.tile([P, PACK, D], BF16)
         nc.sync.dma_start(out=we_raw[:], in_=We.rearrange("(t p) n -> p t n", p=P))
 
@@ -78,10 +70,10 @@ def tile_wavenetworklm_pb_s_kernel(tc, h_r, h_i, w2r, b2r, w2i, b2i, We, be, g_r
         nc.sync.dma_start(out=free_rows[0:1, 0:D], in_=be.rearrange("(o n) -> o n", o=1))
         nc.sync.dma_start(out=free_rows[0:1, D : 2 * D], in_=g_rms.rearrange("(o n) -> o n", o=1))
 
-        sqrt_in = keep.tile([P, 1], F32)
-        sqrt_out = keep.tile([P, 1], F32)
-        nc.vector.memset(sqrt_in[:], 1.0)
-        nc.scalar.activation(out=sqrt_out[:], in_=sqrt_in[:], func=ACT.Sqrt)
+        warm_in = keep.tile([P, 1], F32)
+        warm_out = keep.tile([P, 1], F32)
+        nc.vector.memset(warm_in[:], 1.0)
+        nc.scalar.activation(out=warm_out[:], in_=warm_in[:], func=ACT.Abs_reciprocal_sqrt)
         ones = keep.tile([P, P], BF16)
         nc.vector.memset(ones[:], 1.0)
         ident_f32 = keep.tile([P, P], F32)
@@ -91,54 +83,57 @@ def tile_wavenetworklm_pb_s_kernel(tc, h_r, h_i, w2r, b2r, w2i, b2i, We, be, g_r
 
         xt = {}
         for s, j in units:
-            words = x_sb[s, j][:].bitcast(F32)
-            xt[s, j] = psum_xt.tile([P, PASSES * 2, P], F32, name="xt%d%d" % (s, j), tag="xt")
-            for q in range(PASSES * 2):
-                nc.tensor.transpose(xt[s, j][:, q, :], words[:, P * q : P * (q + 1)], ident_f32[:])
+            words = x_sb[s, j][:].bitcast(F32).rearrange("r (g p u) -> r g u p", g=PASSES, u=2)
+            xt[s, j] = psum_xt.tile([P, PASSES, 2, P], F32, name="xt%d%d" % (s, j), tag="xt")
+            for g in range(PASSES):
+                for u in range(2):
+                    nc.tensor.transpose(xt[s, j][:, g, u, :], words[:, g, u, :], ident_f32[:])
         b2_ps = psum_misc.tile([P, P], BF16, tag="misc")
         nc.tensor.transpose(b2_ps[:], b2_rows[:], ident_bf16[:])
 
-        def interleaved(grouped, raw):
-            return dict(
-                out=grouped[:].rearrange("p (c i) t -> p c t i", i=RUN),
-                in_=raw[:].rearrange("p t (c i) -> p c t i", i=RUN),
+        def interleave(copy, grouped, raw, cols):
+            copy(
+                out=grouped[:, cols, :].rearrange("p (c i) t -> p c t i", i=RUN),
+                in_=raw[:, :, cols].rearrange("p t (c i) -> p c t i", i=RUN),
             )
 
         def quantise(grouped_flat, codes, scales):
             nc.vector.quantize_mx(out=codes.bitcast(FP8X4), scales=scales, in_=grouped_flat)
 
         h_grp = {}
-        for s, j in units:
-            h_grp[s, j] = keep.tile([P, PASSES, P, PACK], BF16, name="h_grp%d%d" % (s, j), align_bytes=64)
-            nc.scalar.copy(
-                out=h_grp[s, j][:].bitcast(F32),
-                in_=xt[s, j][:].rearrange("p (g u) r -> p g r u", u=2),
-            )
-        we_grp = keep.tile([P, D, PACK], BF16, align_bytes=64)
-        nc.scalar.copy(**interleaved(we_grp, we_raw))
-
-        w_codes = keep.tile([P, STREAMS, PASSES, D], U32, align_bytes=64)
-        w_scales = keep.tile([P, STREAMS, PASSES, D], U8, align_bytes=64)
-        for s in range(STREAMS):
-            w_grp = {}
-            for g in range(PASSES):
-                w_grp[g] = keep.tile([P, D, PACK], BF16, name="w_grp%d%d" % (s, g), align_bytes=64)
-                nc.vector.tensor_copy(**interleaved(w_grp[g], w_raw[s, g]))
-            for g in range(PASSES):
-                quantise(w_grp[g][:].rearrange("p c t -> p (c t)"), w_codes[:, s, g, :], w_scales[:, s, g, :])
         h_codes = keep.tile([P, STREAMS, HALVES, PASSES, P], U32, align_bytes=64)
         h_scales = keep.tile([P, STREAMS, HALVES, PASSES, P], U8, align_bytes=64)
-        for s, j in units:
+        w_codes = keep.tile([P, STREAMS, PASSES, D], U32, align_bytes=64)
+        w_scales = keep.tile([P, STREAMS, PASSES, D], U8, align_bytes=64)
+
+        def quantise_tokens(s, j):
             quantise(
                 h_grp[s, j][:].rearrange("p g r t -> p (g r t)"),
                 h_codes[:, s, j, :, :].rearrange("p g r -> p (g r)"),
                 h_scales[:, s, j, :, :].rearrange("p g r -> p (g r)"),
             )
 
+        for i in range(len(units)):
+            s, j = units[i]
+            ws, g = pieces[i]
+            w_grp = keep.tile([P, D, PACK], BF16, name="w_grp%d%d" % (ws, g), align_bytes=64)
+            interleave(nc.scalar.copy, w_grp, w_raw[ws, g], slice(VECTOR_COLS, D))
+            h_grp[s, j] = keep.tile([P, PASSES, P, PACK], BF16, name="h_grp%d%d" % (s, j), align_bytes=64)
+            nc.scalar.copy(out=h_grp[s, j][:].bitcast(F32), in_=xt[s, j][:].rearrange("p g u r -> p g r u"))
+            interleave(nc.vector.tensor_copy, w_grp, w_raw[ws, g], slice(0, VECTOR_COLS))
+            if i > 0:
+                quantise_tokens(*units[i - 1])
+            quantise(w_grp[:].rearrange("p c t -> p (c t)"), w_codes[:, ws, g, :], w_scales[:, ws, g, :])
+        quantise_tokens(*units[-1])
+
+        we_grp = keep.tile([P, D, PACK], BF16, align_bytes=64)
+        interleave(nc.scalar.copy, we_grp, we_raw, slice(0, D))
+
         cat_ps = [
             psum_cat.tile([P, CHUNKS, P], F32, name="cat_ps%d" % j) for j in range(HALVES)
         ]
-        for s, j in units:
+
+        def first_contraction(s, j):
             for cc in range(CHUNKS_PER_STREAM):
                 cols = slice(P * cc, P * (cc + 1))
                 for g in range(PASSES):
@@ -152,12 +147,16 @@ def tile_wavenetworklm_pb_s_kernel(tc, h_r, h_i, w2r, b2r, w2i, b2i, We, be, g_r
                         stop=(g == PASSES - 1),
                     )
 
+        for s in range(STREAMS):
+            first_contraction(s, 0)
         spread_ps = psum_misc.tile([P, 2 * D], F32, tag="misc")
         nc.tensor.matmul(out=spread_ps[:], lhsT=ones[:], rhs=free_rows[:], start=True, stop=True)
         spread = keep.tile([P, 2 * D], F32)
         nc.scalar.copy(out=spread[:], in_=spread_ps[:])
         be_all = spread[:, 0:D]
         g_all = spread[:, D : 2 * D]
+        for s in range(STREAMS):
+            first_contraction(s, 1)
 
         b2_cols = keep.tile([P, CHUNKS], F32)
         nc.vector.tensor_copy(out=b2_cols[:], in_=b2_ps[:, 0:CHUNKS])
@@ -168,7 +167,7 @@ def tile_wavenetworklm_pb_s_kernel(tc, h_r, h_i, w2r, b2r, w2i, b2i, We, be, g_r
         we_scales = keep.tile([P, D], U8, align_bytes=64)
         wave = keep.tile([P, HALVES, D], F32)
         wave_ps = {}
-        rms = {}
+        inv_rms = {}
         out_rows = out.flatten_outer_dims().rearrange("(p j) n -> p j n", j=HALVES)
 
         def add_b2(j):
@@ -199,15 +198,15 @@ def tile_wavenetworklm_pb_s_kernel(tc, h_r, h_i, w2r, b2r, w2i, b2i, We, be, g_r
             squares = keep.tile([P, D], F32, name="squares%d" % j)
             sum_sq = keep.tile([P, 1], F32, name="sum_sq%d" % j)
             nc.scalar.activation(out=squares[:], in_=wave[:, j, :], func=ACT.Square, accum_out=sum_sq[:])
-            rms[j] = keep.tile([P, 1], F32, name="rms%d" % j)
-            nc.scalar.activation(out=rms[j][:], in_=sum_sq[:], func=ACT.Sqrt, scale=1.0 / D, bias=EPS)
+            inv_rms[j] = keep.tile([P, 1], F32, name="inv_rms%d" % j)
+            nc.scalar.activation(
+                out=inv_rms[j][:], in_=sum_sq[:], func=ACT.Abs_reciprocal_sqrt, scale=1.0 / D, bias=EPS
+            )
 
         def normalise_and_store(j):
-            inv_rms = keep.tile([P, 1], F32, name="inv_rms%d" % j)
-            nc.vector.reciprocal(out=inv_rms[:], in_=rms[j][:])
             normed = keep.tile([P, D], F32, name="normed%d" % j)
             nc.vector.scalar_tensor_tensor(
-                out=normed[:], in0=wave[:, j, :], scalar=inv_rms[:, 0:1], in1=g_all, op0=MULT, op1=MULT
+                out=normed[:], in0=wave[:, j, :], scalar=inv_rms[j][:, 0:1], in1=g_all, op0=MULT, op1=MULT
             )
             nc.sync.dma_start(out=out_rows[:, j, :], in_=normed[:])
 
@@ -215,8 +214,8 @@ def tile_wavenetworklm_pb_s_kernel(tc, h_r, h_i, w2r, b2r, w2i, b2i, We, be, g_r
         quantise(we_grp[:].rearrange("p n t -> p (n t)"), we_codes[:], we_scales[:])
         second_contraction(0)
         add_b2(1)
-        add_be_and_measure(0)
         second_contraction(1)
-        add_be_and_measure(1)
-        normalise_and_store(0)
-        normalise_and_store(1)
+        for j in range(HALVES):
+            add_be_and_measure(j)
+        for j in range(HALVES):
+            normalise_and_store(j)

@@ -26,7 +26,8 @@ PASSES = HID // K_PASS
 CHUNKS = D2 // P
 CHUNKS_PER_STREAM = D // P
 RUN = 4
-VECTOR_COLS = 176
+W_VECTOR_COLS = 176
+WE_VECTOR_COLS = 64
 
 FLOPS = 2 * TOKENS * HID * D * STREAMS + 2 * TOKENS * D2 * D
 
@@ -36,28 +37,45 @@ def tile_wavenetworklm_pb_s_kernel(tc, h_r, h_i, w2r, b2r, w2i, b2i, We, be, g_r
     hidden = (h_r, h_i)
     weights = (w2r, w2i)
     biases = (b2r, b2i)
-    units = [(s, j) for j in range(HALVES) for s in range(STREAMS)]
-    pieces = [(s, g) for s in range(STREAMS) for g in range(PASSES)]
 
     with ExitStack() as ctx:
         keep = ctx.enter_context(tc.tile_pool(name="keep", bufs=1))
-        psum_xt = ctx.enter_context(tc.psum_pool(name="psum_xt", bufs=len(units)))
+        psum_xt = ctx.enter_context(tc.psum_pool(name="psum_xt", bufs=STREAMS * HALVES))
         psum_cat = ctx.enter_context(tc.psum_pool(name="psum_cat", bufs=1))
         psum_misc = ctx.enter_context(tc.psum_pool(name="psum_misc", bufs=2))
         ctx.enter_context(tc.manual_schedule())
 
         x_sb = {}
         w_raw = {}
-        for (s, j), (ws, g) in zip(units, pieces):
-            tokens = hidden[s].flatten_outer_dims().rearrange("(p j) k -> p j k", j=HALVES)
-            x_sb[s, j] = keep.tile([P, HID], BF16, name="x_sb%d%d" % (s, j))
-            nc.sync.dma_start(out=x_sb[s, j][:], in_=tokens[:, j, :])
-            rows = weights[ws].rearrange("(g p t) c -> g p t c", g=PASSES, p=P, t=PACK)
-            w_raw[ws, g] = keep.tile([P, PACK, D], BF16, name="w_raw%d%d" % (ws, g))
-            nc.sync.dma_start(out=w_raw[ws, g][:], in_=rows[g])
-        we_raw = keep.tile([P, PACK, D], BF16)
-        nc.sync.dma_start(out=we_raw[:], in_=We.rearrange("(t p) n -> p t n", p=P))
 
+        def token_rows(s, j):
+            return hidden[s].flatten_outer_dims().rearrange("(p j) k -> p j k", j=HALVES)[:, j, :]
+
+        def load_unit(s, j):
+            whole = keep.tile([P, HID], BF16, name="x_sb%d%d" % (s, j))
+            nc.sync.dma_start(out=whole[:], in_=token_rows(s, j))
+            for g in range(PASSES):
+                x_sb[s, j, g] = whole[:, K_PASS * g : K_PASS * (g + 1)]
+
+        def load_unit_pass(s, j, g):
+            part = keep.tile([P, K_PASS], BF16, name="x_sb%d%d%d" % (s, j, g))
+            nc.sync.dma_start(out=part[:], in_=token_rows(s, j)[:, K_PASS * g : K_PASS * (g + 1)])
+            x_sb[s, j, g] = part[:]
+
+        def load_piece(s, g):
+            rows = weights[s].rearrange("(g p t) c -> g p t c", g=PASSES, p=P, t=PACK)
+            w_raw[s, g] = keep.tile([P, PACK, D], BF16, name="w_raw%d%d" % (s, g))
+            nc.sync.dma_start(out=w_raw[s, g][:], in_=rows[g])
+
+        load_unit(0, 0)
+        load_piece(0, 0)
+        load_unit(1, 0)
+        load_piece(0, 1)
+        load_unit(0, 1)
+        load_piece(1, 0)
+        load_piece(1, 1)
+        for g in range(PASSES):
+            load_unit_pass(1, 1, g)
         b2_rows = keep.tile([P, P], BF16)
         nc.vector.memset(b2_rows[:], 0.0)
         free_rows = keep.tile([P, 2 * D], BF16)
@@ -67,6 +85,8 @@ def tile_wavenetworklm_pb_s_kernel(tc, h_r, h_i, w2r, b2r, w2i, b2i, We, be, g_r
                 out=b2_rows[CHUNKS_PER_STREAM * s : CHUNKS_PER_STREAM * (s + 1), :],
                 in_=biases[s].rearrange("(c p) -> c p", p=P),
             )
+        we_raw = keep.tile([P, PACK, D], BF16)
+        nc.sync.dma_start(out=we_raw[:], in_=We.rearrange("(t p) n -> p t n", p=P))
         nc.sync.dma_start(out=free_rows[0:1, 0:D], in_=be.rearrange("(o n) -> o n", o=1))
         nc.sync.dma_start(out=free_rows[0:1, D : 2 * D], in_=g_rms.rearrange("(o n) -> o n", o=1))
 
@@ -81,15 +101,49 @@ def tile_wavenetworklm_pb_s_kernel(tc, h_r, h_i, w2r, b2r, w2i, b2i, We, be, g_r
         ident_bf16 = keep.tile([P, P], BF16)
         make_identity(nc, ident_bf16[:])
 
-        xt = {}
-        for s, j in units:
-            words = x_sb[s, j][:].bitcast(F32).rearrange("r (g p u) -> r g u p", g=PASSES, u=2)
-            xt[s, j] = psum_xt.tile([P, PASSES, 2, P], F32, name="xt%d%d" % (s, j), tag="xt")
+        h_grp = {}
+        for j in range(HALVES):
+            for s in range(STREAMS):
+                h_grp[s, j] = keep.tile([P, PASSES, P, PACK], BF16, name="h_grp%d%d" % (s, j), align_bytes=64)
+        w_grp = {}
+        for s in range(STREAMS):
             for g in range(PASSES):
+                w_grp[s, g] = keep.tile([P, D, PACK], BF16, name="w_grp%d%d" % (s, g), align_bytes=64)
+        we_grp = keep.tile([P, D, PACK], BF16, align_bytes=64)
+        h_codes = keep.tile([P, STREAMS, HALVES, PASSES, P], U32, align_bytes=64)
+        h_scales = keep.tile([P, STREAMS, HALVES, PASSES, P], U8, align_bytes=64)
+        w_codes = keep.tile([P, STREAMS, PASSES, D], U32, align_bytes=64)
+        w_scales = keep.tile([P, STREAMS, PASSES, D], U8, align_bytes=64)
+        b2_cols = keep.tile([P, CHUNKS], F32)
+        cat_ps = [
+            psum_cat.tile([P, CHUNKS, P], F32, name="cat_ps%d" % j) for j in range(HALVES)
+        ]
+        cat_grp = keep.tile([P, HALVES, P, CHUNKS], BF16, align_bytes=64)
+        cat_codes = keep.tile([P, HALVES, P], U32, align_bytes=64)
+        cat_scales = keep.tile([P, HALVES, P], U8, align_bytes=64)
+        we_codes = keep.tile([P, D], U32, align_bytes=64)
+        we_scales = keep.tile([P, D], U8, align_bytes=64)
+        wave = keep.tile([P, HALVES, D], F32)
+        spread = keep.tile([P, 2 * D], F32)
+        be_all = spread[:, 0:D]
+        g_all = spread[:, D : 2 * D]
+        wave_ps = {}
+        sum_sq = {}
+        inv_rms = {}
+        out_rows = out.flatten_outer_dims().rearrange("(p j) n -> p j n", j=HALVES)
+
+        def transpose_tokens(s, j, passes):
+            xt = psum_xt.tile([P, len(passes), 2, P], F32, name="xt%d%d%d" % (s, j, passes[0]), tag="xt")
+            for i, g in enumerate(passes):
+                words = x_sb[s, j, g].bitcast(F32).rearrange("r (p u) -> r u p", u=2)
                 for u in range(2):
-                    nc.tensor.transpose(xt[s, j][:, g, u, :], words[:, g, u, :], ident_f32[:])
-        b2_ps = psum_misc.tile([P, P], BF16, tag="misc")
-        nc.tensor.transpose(b2_ps[:], b2_rows[:], ident_bf16[:])
+                    nc.tensor.transpose(xt[:, i, u, :], words[:, u, :], ident_f32[:])
+            return xt
+
+        def regroup_tokens(s, j, passes, xt):
+            nc.scalar.copy(
+                out=h_grp[s, j][:, passes[0] : passes[-1] + 1, :, :].bitcast(F32), in_=xt[:].rearrange("p g u r -> p g r u")
+            )
 
         def interleave(copy, grouped, raw, cols):
             copy(
@@ -97,14 +151,14 @@ def tile_wavenetworklm_pb_s_kernel(tc, h_r, h_i, w2r, b2r, w2i, b2i, We, be, g_r
                 in_=raw[:, :, cols].rearrange("p t (c i) -> p c t i", i=RUN),
             )
 
+        def interleave_on_vector(s, g):
+            interleave(nc.vector.tensor_copy, w_grp[s, g], w_raw[s, g], slice(0, W_VECTOR_COLS))
+
+        def interleave_on_scalar(s, g):
+            interleave(nc.scalar.copy, w_grp[s, g], w_raw[s, g], slice(W_VECTOR_COLS, D))
+
         def quantise(grouped_flat, codes, scales):
             nc.vector.quantize_mx(out=codes.bitcast(FP8X4), scales=scales, in_=grouped_flat)
-
-        h_grp = {}
-        h_codes = keep.tile([P, STREAMS, HALVES, PASSES, P], U32, align_bytes=64)
-        h_scales = keep.tile([P, STREAMS, HALVES, PASSES, P], U8, align_bytes=64)
-        w_codes = keep.tile([P, STREAMS, PASSES, D], U32, align_bytes=64)
-        w_scales = keep.tile([P, STREAMS, PASSES, D], U8, align_bytes=64)
 
         def quantise_tokens(s, j):
             quantise(
@@ -113,25 +167,8 @@ def tile_wavenetworklm_pb_s_kernel(tc, h_r, h_i, w2r, b2r, w2i, b2i, We, be, g_r
                 h_scales[:, s, j, :, :].rearrange("p g r -> p (g r)"),
             )
 
-        for i in range(len(units)):
-            s, j = units[i]
-            ws, g = pieces[i]
-            w_grp = keep.tile([P, D, PACK], BF16, name="w_grp%d%d" % (ws, g), align_bytes=64)
-            interleave(nc.scalar.copy, w_grp, w_raw[ws, g], slice(VECTOR_COLS, D))
-            h_grp[s, j] = keep.tile([P, PASSES, P, PACK], BF16, name="h_grp%d%d" % (s, j), align_bytes=64)
-            nc.scalar.copy(out=h_grp[s, j][:].bitcast(F32), in_=xt[s, j][:].rearrange("p g u r -> p g r u"))
-            interleave(nc.vector.tensor_copy, w_grp, w_raw[ws, g], slice(0, VECTOR_COLS))
-            if i > 0:
-                quantise_tokens(*units[i - 1])
-            quantise(w_grp[:].rearrange("p c t -> p (c t)"), w_codes[:, ws, g, :], w_scales[:, ws, g, :])
-        quantise_tokens(*units[-1])
-
-        we_grp = keep.tile([P, D, PACK], BF16, align_bytes=64)
-        interleave(nc.scalar.copy, we_grp, we_raw, slice(0, D))
-
-        cat_ps = [
-            psum_cat.tile([P, CHUNKS, P], F32, name="cat_ps%d" % j) for j in range(HALVES)
-        ]
+        def quantise_weights(s, g):
+            quantise(w_grp[s, g][:].rearrange("p c t -> p (c t)"), w_codes[:, s, g, :], w_scales[:, s, g, :])
 
         def first_contraction(s, j):
             for cc in range(CHUNKS_PER_STREAM):
@@ -147,29 +184,6 @@ def tile_wavenetworklm_pb_s_kernel(tc, h_r, h_i, w2r, b2r, w2i, b2i, We, be, g_r
                         stop=(g == PASSES - 1),
                     )
 
-        for s in range(STREAMS):
-            first_contraction(s, 0)
-        spread_ps = psum_misc.tile([P, 2 * D], F32, tag="misc")
-        nc.tensor.matmul(out=spread_ps[:], lhsT=ones[:], rhs=free_rows[:], start=True, stop=True)
-        spread = keep.tile([P, 2 * D], F32)
-        nc.scalar.copy(out=spread[:], in_=spread_ps[:])
-        be_all = spread[:, 0:D]
-        g_all = spread[:, D : 2 * D]
-        for s in range(STREAMS):
-            first_contraction(s, 1)
-
-        b2_cols = keep.tile([P, CHUNKS], F32)
-        nc.vector.tensor_copy(out=b2_cols[:], in_=b2_ps[:, 0:CHUNKS])
-        cat_grp = keep.tile([P, HALVES, P, CHUNKS], BF16, align_bytes=64)
-        cat_codes = keep.tile([P, HALVES, P], U32, align_bytes=64)
-        cat_scales = keep.tile([P, HALVES, P], U8, align_bytes=64)
-        we_codes = keep.tile([P, D], U32, align_bytes=64)
-        we_scales = keep.tile([P, D], U8, align_bytes=64)
-        wave = keep.tile([P, HALVES, D], F32)
-        wave_ps = {}
-        inv_rms = {}
-        out_rows = out.flatten_outer_dims().rearrange("(p j) n -> p j n", j=HALVES)
-
         def add_b2(j):
             nc.vector.tensor_tensor(
                 out=cat_grp[:, j, :, :],
@@ -178,10 +192,12 @@ def tile_wavenetworklm_pb_s_kernel(tc, h_r, h_i, w2r, b2r, w2i, b2i, We, be, g_r
                 op=ADD,
             )
 
-        def second_contraction(j):
+        def quantise_cat(j):
             quantise(
                 cat_grp[:, j, :, :].rearrange("p r c -> p (r c)"), cat_codes[:, j, :], cat_scales[:, j, :]
             )
+
+        def second_contraction(j):
             wave_ps[j] = psum_misc.tile([P, D], F32, name="wave_ps%d" % j, tag="misc")
             nc.tensor.matmul_mx(
                 out=wave_ps[j][:],
@@ -193,29 +209,73 @@ def tile_wavenetworklm_pb_s_kernel(tc, h_r, h_i, w2r, b2r, w2i, b2i, We, be, g_r
                 stop=True,
             )
 
-        def add_be_and_measure(j):
+        def add_be(j):
             nc.vector.tensor_tensor(out=wave[:, j, :], in0=wave_ps[j][:], in1=be_all, op=ADD)
+
+        def measure(j):
             squares = keep.tile([P, D], F32, name="squares%d" % j)
-            sum_sq = keep.tile([P, 1], F32, name="sum_sq%d" % j)
-            nc.scalar.activation(out=squares[:], in_=wave[:, j, :], func=ACT.Square, accum_out=sum_sq[:])
+            sum_sq[j] = keep.tile([P, 1], F32, name="sum_sq%d" % j)
+            nc.scalar.activation(out=squares[:], in_=wave[:, j, :], func=ACT.Square, accum_out=sum_sq[j][:])
             inv_rms[j] = keep.tile([P, 1], F32, name="inv_rms%d" % j)
             nc.scalar.activation(
-                out=inv_rms[j][:], in_=sum_sq[:], func=ACT.Abs_reciprocal_sqrt, scale=1.0 / D, bias=EPS
+                out=inv_rms[j][:], in_=sum_sq[j][:], func=ACT.Abs_reciprocal_sqrt, scale=1.0 / D, bias=EPS
             )
 
-        def normalise_and_store(j):
+        both = range(PASSES)
+        xt00 = transpose_tokens(0, 0, both)
+        interleave_on_vector(0, 0)
+        interleave_on_scalar(0, 0)
+        regroup_tokens(0, 0, both, xt00)
+        quantise_weights(0, 0)
+
+        xt10 = transpose_tokens(1, 0, both)
+        interleave_on_vector(0, 1)
+        interleave_on_scalar(0, 1)
+        quantise_tokens(0, 0)
+        regroup_tokens(1, 0, both, xt10)
+        quantise_weights(0, 1)
+
+        xt01 = transpose_tokens(0, 1, both)
+        first_contraction(0, 0)
+        interleave_on_vector(1, 0)
+        interleave_on_scalar(1, 0)
+        quantise_tokens(1, 0)
+
+        interleave_on_vector(1, 1)
+        interleave_on_scalar(1, 1)
+        regroup_tokens(0, 1, both, xt01)
+        quantise_weights(1, 0)
+        quantise_weights(1, 1)
+        quantise_tokens(0, 1)
+
+        for g in range(PASSES):
+            xt11 = transpose_tokens(1, 1, [g])
+            regroup_tokens(1, 1, [g], xt11)
+        b2_ps = psum_misc.tile([P, P], BF16, tag="misc")
+        nc.tensor.transpose(b2_ps[:], b2_rows[:], ident_bf16[:])
+        nc.vector.tensor_copy(out=b2_cols[:], in_=b2_ps[:, 0:CHUNKS])
+        interleave(nc.vector.tensor_copy, we_grp, we_raw, slice(0, WE_VECTOR_COLS))
+        interleave(nc.scalar.copy, we_grp, we_raw, slice(WE_VECTOR_COLS, D))
+        first_contraction(1, 0)
+        first_contraction(0, 1)
+        quantise_tokens(1, 1)
+        first_contraction(1, 1)
+        spread_ps = psum_misc.tile([P, 2 * D], F32, tag="misc")
+        nc.tensor.matmul(out=spread_ps[:], lhsT=ones[:], rhs=free_rows[:], start=True, stop=True)
+        nc.scalar.copy(out=spread[:], in_=spread_ps[:])
+
+        add_b2(0)
+        quantise(we_grp[:].rearrange("p n t -> p (n t)"), we_codes[:], we_scales[:])
+        add_b2(1)
+        for j in range(HALVES):
+            quantise_cat(j)
+            second_contraction(j)
+        for j in range(HALVES):
+            add_be(j)
+            measure(j)
+        for j in range(HALVES):
             normed = keep.tile([P, D], F32, name="normed%d" % j)
             nc.vector.scalar_tensor_tensor(
                 out=normed[:], in0=wave[:, j, :], scalar=inv_rms[j][:, 0:1], in1=g_all, op0=MULT, op1=MULT
             )
             nc.sync.dma_start(out=out_rows[:, j, :], in_=normed[:])
-
-        add_b2(0)
-        quantise(we_grp[:].rearrange("p n t -> p (n t)"), we_codes[:], we_scales[:])
-        second_contraction(0)
-        add_b2(1)
-        second_contraction(1)
-        for j in range(HALVES):
-            add_be_and_measure(j)
-        for j in range(HALVES):
-            normalise_and_store(j)

@@ -40,9 +40,7 @@ def tile_wavenetworklm_pb_s_kernel(tc, h_r, h_i, w2r, b2r, w2i, b2i, We, be, g_r
 
     with ExitStack() as ctx:
         keep = ctx.enter_context(tc.tile_pool(name="keep", bufs=1))
-        psum_xt = ctx.enter_context(tc.psum_pool(name="psum_xt", bufs=STREAMS * HALVES))
-        psum_cat = ctx.enter_context(tc.psum_pool(name="psum_cat", bufs=1))
-        psum_misc = ctx.enter_context(tc.psum_pool(name="psum_misc", bufs=2))
+        psum = ctx.enter_context(tc.psum_pool(name="psum", bufs=1))
         ctx.enter_context(tc.manual_schedule())
 
         x_sb = {}
@@ -116,7 +114,7 @@ def tile_wavenetworklm_pb_s_kernel(tc, h_r, h_i, w2r, b2r, w2i, b2i, We, be, g_r
         w_scales = keep.tile([P, STREAMS, PASSES, D], U8, align_bytes=64)
         b2_cols = keep.tile([P, CHUNKS], F32)
         cat_ps = [
-            psum_cat.tile([P, CHUNKS, P], F32, name="cat_ps%d" % j) for j in range(HALVES)
+            psum.tile([P, CHUNKS, P], F32, name="cat_ps%d" % j, tag="cat%d" % j) for j in range(HALVES)
         ]
         cat_grp = keep.tile([P, HALVES, P, CHUNKS], BF16, align_bytes=64)
         cat_codes = keep.tile([P, HALVES, P], U32, align_bytes=64)
@@ -133,7 +131,8 @@ def tile_wavenetworklm_pb_s_kernel(tc, h_r, h_i, w2r, b2r, w2i, b2i, We, be, g_r
         out_rows = out.flatten_outer_dims().rearrange("(p j) n -> p j n", j=HALVES)
 
         def transpose_tokens(s, j, passes):
-            xt = psum_xt.tile([P, len(passes), 2, P], F32, name="xt%d%d%d" % (s, j, passes[0]), tag="xt")
+            name = "xt%d%d%d" % (s, j, passes[0])
+            xt = psum.tile([P, len(passes), 2, P], F32, name=name, tag=name)
             for i, g in enumerate(passes):
                 words = x_sb[s, j, g].bitcast(F32).rearrange("r (p u) -> r u p", u=2)
                 for u in range(2):
@@ -198,7 +197,7 @@ def tile_wavenetworklm_pb_s_kernel(tc, h_r, h_i, w2r, b2r, w2i, b2i, We, be, g_r
             )
 
         def second_contraction(j):
-            wave_ps[j] = psum_misc.tile([P, D], F32, name="wave_ps%d" % j, tag="misc")
+            wave_ps[j] = psum.tile([P, D], F32, name="wave_ps%d" % j, tag=("b2", "cat0")[j])
             nc.tensor.matmul_mx(
                 out=wave_ps[j][:],
                 lhsT=cat_codes[:, j, :].bitcast(FP8X4),
@@ -251,7 +250,7 @@ def tile_wavenetworklm_pb_s_kernel(tc, h_r, h_i, w2r, b2r, w2i, b2i, We, be, g_r
         for g in range(PASSES):
             xt11 = transpose_tokens(1, 1, [g])
             regroup_tokens(1, 1, [g], xt11)
-        b2_ps = psum_misc.tile([P, P], BF16, tag="misc")
+        b2_ps = psum.tile([P, P], BF16, tag="b2")
         nc.tensor.transpose(b2_ps[:], b2_rows[:], ident_bf16[:])
         nc.vector.tensor_copy(out=b2_cols[:], in_=b2_ps[:, 0:CHUNKS])
         interleave(nc.vector.tensor_copy, we_grp, we_raw, slice(0, WE_VECTOR_COLS))
@@ -260,16 +259,17 @@ def tile_wavenetworklm_pb_s_kernel(tc, h_r, h_i, w2r, b2r, w2i, b2i, We, be, g_r
         first_contraction(0, 1)
         quantise_tokens(1, 1)
         first_contraction(1, 1)
-        spread_ps = psum_misc.tile([P, 2 * D], F32, tag="misc")
+        spread_ps = psum.tile([P, 2 * D], F32, tag="xt000")
         nc.tensor.matmul(out=spread_ps[:], lhsT=ones[:], rhs=free_rows[:], start=True, stop=True)
         nc.scalar.copy(out=spread[:], in_=spread_ps[:])
 
         add_b2(0)
         quantise(we_grp[:].rearrange("p n t -> p (n t)"), we_codes[:], we_scales[:])
+        quantise_cat(0)
+        second_contraction(0)
         add_b2(1)
-        for j in range(HALVES):
-            quantise_cat(j)
-            second_contraction(j)
+        quantise_cat(1)
+        second_contraction(1)
         for j in range(HALVES):
             add_be(j)
             measure(j)

@@ -25,7 +25,7 @@ HALVES = TOKENS // P
 PASSES = HID // K_PASS
 CHUNKS = D2 // P
 CHUNKS_PER_STREAM = D // P
-RUN = 4
+RUN = 8
 W_VECTOR_COLS = 176
 WE_VECTOR_COLS = 64
 

@@ -47,7 +47,7 @@ def tile_wavenetworklm_pb_s_kernel(tc, h_r, h_i, w2r, b2r, w2i, b2i, We, be, g_r
         w_raw = {}
 
         def token_rows(s, j):
-            return hidden[s].flatten_outer_dims().rearrange("(p j) k -> p j k", j=HALVES)[:, j, :]
+            return hidden[s].flatten_outer_dims().rearrange("(j p) k -> p j k", j=HALVES)[:, j, :]
 
         def load_unit(s, j):
             whole = keep.tile([P, HID], BF16, name="x_sb%d%d" % (s, j))
@@ -128,7 +128,7 @@ def tile_wavenetworklm_pb_s_kernel(tc, h_r, h_i, w2r, b2r, w2i, b2i, We, be, g_r
         wave_ps = {}
         sum_sq = {}
         inv_rms = {}
-        out_rows = out.flatten_outer_dims().rearrange("(p j) n -> p j n", j=HALVES)
+        out_rows = out.flatten_outer_dims().rearrange("(j p) n -> p j n", j=HALVES)
 
         def transpose_tokens(s, j, passes):
             name = "xt%d%d%d" % (s, j, passes[0])

from contextlib import ExitStack

import concourse.mybir as mybir
from concourse.masks import make_identity

F32 = mybir.dt.float32
BF16 = mybir.dt.bfloat16
U32 = mybir.dt.uint32
U8 = mybir.dt.uint8
FP8X4 = mybir.dt.float8_e4m3fn_x4
ADD = mybir.AluOpType.add
MULT = mybir.AluOpType.mult
ACT = mybir.ActivationFunctionType

P = 128
PACK = 4
K_PASS = P * PACK
TOKENS = 256
HID = 1024
D = 256
D2 = 2 * D
EPS = 1e-6
STREAMS = 2
HALVES = TOKENS // P
PASSES = HID // K_PASS
CHUNKS = D2 // P
CHUNKS_PER_STREAM = D // P
RUN = 8
W_VECTOR_COLS = 176
WE_VECTOR_COLS = 64

FLOPS = 2 * TOKENS * HID * D * STREAMS + 2 * TOKENS * D2 * D


def tile_wavenetworklm_pb_s_kernel(tc, h_r, h_i, w2r, b2r, w2i, b2i, We, be, g_rms, out):
    nc = tc.nc
    hidden = (h_r, h_i)
    weights = (w2r, w2i)
    biases = (b2r, b2i)

    with ExitStack() as ctx:
        keep = ctx.enter_context(tc.tile_pool(name="keep", bufs=1))
        psum = ctx.enter_context(tc.psum_pool(name="psum", bufs=1))
        ctx.enter_context(tc.manual_schedule())

        x_sb = {}
        w_raw = {}

        def token_rows(s, j):
            return hidden[s].flatten_outer_dims().rearrange("(j p) k -> p j k", j=HALVES)[:, j, :]

        def load_unit(s, j):
            whole = keep.tile([P, HID], BF16, name="x_sb%d%d" % (s, j))
            nc.sync.dma_start(out=whole[:], in_=token_rows(s, j))
            for g in range(PASSES):
                x_sb[s, j, g] = whole[:, K_PASS * g : K_PASS * (g + 1)]

        def load_unit_pass(s, j, g):
            part = keep.tile([P, K_PASS], BF16, name="x_sb%d%d%d" % (s, j, g))
            nc.sync.dma_start(out=part[:], in_=token_rows(s, j)[:, K_PASS * g : K_PASS * (g + 1)])
            x_sb[s, j, g] = part[:]

        def load_piece(s, g):
            rows = weights[s].rearrange("(g p t) c -> g p t c", g=PASSES, p=P, t=PACK)
            w_raw[s, g] = keep.tile([P, PACK, D], BF16, name="w_raw%d%d" % (s, g))
            nc.sync.dma_start(out=w_raw[s, g][:], in_=rows[g])

        load_unit(0, 0)
        load_piece(0, 0)
        load_unit(1, 0)
        load_piece(0, 1)
        load_unit(0, 1)
        load_piece(1, 0)
        load_piece(1, 1)
        for g in range(PASSES):
            load_unit_pass(1, 1, g)
        b2_rows = keep.tile([P, P], BF16)
        nc.vector.memset(b2_rows[:], 0.0)
        free_rows = keep.tile([P, 2 * D], BF16)
        nc.vector.memset(free_rows[:], 0.0)
        for s in range(STREAMS):
            nc.sync.dma_start(
                out=b2_rows[CHUNKS_PER_STREAM * s : CHUNKS_PER_STREAM * (s + 1), :],
                in_=biases[s].rearrange("(c p) -> c p", p=P),
            )
        we_raw = keep.tile([P, PACK, D], BF16)
        nc.sync.dma_start(out=we_raw[:], in_=We.rearrange("(t p) n -> p t n", p=P))
        nc.sync.dma_start(out=free_rows[0:1, 0:D], in_=be.rearrange("(o n) -> o n", o=1))
        nc.sync.dma_start(out=free_rows[0:1, D : 2 * D], in_=g_rms.rearrange("(o n) -> o n", o=1))

        warm_in = keep.tile([P, 1], F32)
        warm_out = keep.tile([P, 1], F32)
        nc.vector.memset(warm_in[:], 1.0)
        nc.scalar.activation(out=warm_out[:], in_=warm_in[:], func=ACT.Abs_reciprocal_sqrt)
        ones = keep.tile([P, P], BF16)
        nc.vector.memset(ones[:], 1.0)
        ident_f32 = keep.tile([P, P], F32)
        make_identity(nc, ident_f32[:])
        ident_bf16 = keep.tile([P, P], BF16)
        make_identity(nc, ident_bf16[:])

        h_grp = {}
        for j in range(HALVES):
            for s in range(STREAMS):
                h_grp[s, j] = keep.tile([P, PASSES, P, PACK], BF16, name="h_grp%d%d" % (s, j), align_bytes=64)
        w_grp = {}
        for s in range(STREAMS):
            for g in range(PASSES):
                w_grp[s, g] = keep.tile([P, D, PACK], BF16, name="w_grp%d%d" % (s, g), align_bytes=64)
        we_grp = keep.tile([P, D, PACK], BF16, align_bytes=64)
        h_codes = keep.tile([P, STREAMS, HALVES, PASSES, P], U32, align_bytes=64)
        h_scales = keep.tile([P, STREAMS, HALVES, PASSES, P], U8, align_bytes=64)
        w_codes = keep.tile([P, STREAMS, PASSES, D], U32, align_bytes=64)
        w_scales = keep.tile([P, STREAMS, PASSES, D], U8, align_bytes=64)
        b2_cols = keep.tile([P, CHUNKS], F32)
        cat_ps = [
            psum.tile([P, CHUNKS, P], F32, name="cat_ps%d" % j, tag="cat%d" % j) for j in range(HALVES)
        ]
        cat_grp = keep.tile([P, HALVES, P, CHUNKS], BF16, align_bytes=64)
        cat_codes = keep.tile([P, HALVES, P], U32, align_bytes=64)
        cat_scales = keep.tile([P, HALVES, P], U8, align_bytes=64)
        we_codes = keep.tile([P, D], U32, align_bytes=64)
        we_scales = keep.tile([P, D], U8, align_bytes=64)
        wave = keep.tile([P, HALVES, D], F32)
        spread = keep.tile([P, 2 * D], F32)
        be_all = spread[:, 0:D]
        g_all = spread[:, D : 2 * D]
        wave_ps = {}
        sum_sq = {}
        inv_rms = {}
        out_rows = out.flatten_outer_dims().rearrange("(j p) n -> p j n", j=HALVES)

        def transpose_tokens(s, j, passes):
            name = "xt%d%d%d" % (s, j, passes[0])
            xt = psum.tile([P, len(passes), 2, P], F32, name=name, tag=name)
            for i, g in enumerate(passes):
                words = x_sb[s, j, g].bitcast(F32).rearrange("r (p u) -> r u p", u=2)
                for u in range(2):
                    nc.tensor.transpose(xt[:, i, u, :], words[:, u, :], ident_f32[:])
            return xt

        def regroup_tokens(s, j, passes, xt):
            nc.scalar.copy(
                out=h_grp[s, j][:, passes[0] : passes[-1] + 1, :, :].bitcast(F32), in_=xt[:].rearrange("p g u r -> p g r u")
            )

        def interleave(copy, grouped, raw, cols):
            copy(
                out=grouped[:, cols, :].rearrange("p (c i) t -> p c t i", i=RUN),
                in_=raw[:, :, cols].rearrange("p t (c i) -> p c t i", i=RUN),
            )

        def interleave_on_vector(s, g):
            interleave(nc.vector.tensor_copy, w_grp[s, g], w_raw[s, g], slice(0, W_VECTOR_COLS))

        def interleave_on_scalar(s, g):
            interleave(nc.scalar.copy, w_grp[s, g], w_raw[s, g], slice(W_VECTOR_COLS, D))

        def quantise(grouped_flat, codes, scales):
            nc.vector.quantize_mx(out=codes.bitcast(FP8X4), scales=scales, in_=grouped_flat)

        def quantise_tokens(s, j):
            quantise(
                h_grp[s, j][:].rearrange("p g r t -> p (g r t)"),
                h_codes[:, s, j, :, :].rearrange("p g r -> p (g r)"),
                h_scales[:, s, j, :, :].rearrange("p g r -> p (g r)"),
            )

        def quantise_weights(s, g):
            quantise(w_grp[s, g][:].rearrange("p c t -> p (c t)"), w_codes[:, s, g, :], w_scales[:, s, g, :])

        def first_contraction(s, j):
            for cc in range(CHUNKS_PER_STREAM):
                cols = slice(P * cc, P * (cc + 1))
                for g in range(PASSES):
                    nc.tensor.matmul_mx(
                        out=cat_ps[j][:, CHUNKS_PER_STREAM * s + cc, :],
                        lhsT=w_codes[:, s, g, cols].bitcast(FP8X4),
                        lhsT_scale=w_scales[:, s, g, cols],
                        rhs=h_codes[:, s, j, g, :].bitcast(FP8X4),
                        rhs_scale=h_scales[:, s, j, g, :],
                        start=(g == 0),
                        stop=(g == PASSES - 1),
                    )

        def add_b2(j):
            nc.vector.tensor_tensor(
                out=cat_grp[:, j, :, :],
                in0=cat_ps[j][:].rearrange("p c r -> p r c"),
                in1=b2_cols[:].unsqueeze(1).to_broadcast([P, P, CHUNKS]),
                op=ADD,
            )

        def quantise_cat(j):
            quantise(
                cat_grp[:, j, :, :].rearrange("p r c -> p (r c)"), cat_codes[:, j, :], cat_scales[:, j, :]
            )

        def second_contraction(j):
            wave_ps[j] = psum.tile([P, D], F32, name="wave_ps%d" % j, tag=("b2", "cat0")[j])
            nc.tensor.matmul_mx(
                out=wave_ps[j][:],
                lhsT=cat_codes[:, j, :].bitcast(FP8X4),
                lhsT_scale=cat_scales[:, j, :],
                rhs=we_codes[:].bitcast(FP8X4),
                rhs_scale=we_scales[:],
                start=True,
                stop=True,
            )

        def add_be(j):
            nc.vector.tensor_tensor(out=wave[:, j, :], in0=wave_ps[j][:], in1=be_all, op=ADD)

        def measure(j):
            squares = keep.tile([P, D], F32, name="squares%d" % j)
            sum_sq[j] = keep.tile([P, 1], F32, name="sum_sq%d" % j)
            nc.scalar.activation(out=squares[:], in_=wave[:, j, :], func=ACT.Square, accum_out=sum_sq[j][:])
            inv_rms[j] = keep.tile([P, 1], F32, name="inv_rms%d" % j)
            nc.scalar.activation(
                out=inv_rms[j][:], in_=sum_sq[j][:], func=ACT.Abs_reciprocal_sqrt, scale=1.0 / D, bias=EPS
            )

        both = range(PASSES)
        xt00 = transpose_tokens(0, 0, both)
        interleave_on_vector(0, 0)
        interleave_on_scalar(0, 0)
        regroup_tokens(0, 0, both, xt00)
        quantise_weights(0, 0)

        xt10 = transpose_tokens(1, 0, both)
        interleave_on_vector(0, 1)
        interleave_on_scalar(0, 1)
        quantise_tokens(0, 0)
        regroup_tokens(1, 0, both, xt10)
        quantise_weights(0, 1)

        xt01 = transpose_tokens(0, 1, both)
        first_contraction(0, 0)
        interleave_on_vector(1, 0)
        interleave_on_scalar(1, 0)
        quantise_tokens(1, 0)

        interleave_on_vector(1, 1)
        interleave_on_scalar(1, 1)
        regroup_tokens(0, 1, both, xt01)
        quantise_weights(1, 0)
        quantise_weights(1, 1)
        quantise_tokens(0, 1)

        for g in range(PASSES):
            xt11 = transpose_tokens(1, 1, [g])
            regroup_tokens(1, 1, [g], xt11)
        b2_ps = psum.tile([P, P], BF16, tag="b2")
        nc.tensor.transpose(b2_ps[:], b2_rows[:], ident_bf16[:])
        nc.vector.tensor_copy(out=b2_cols[:], in_=b2_ps[:, 0:CHUNKS])
        interleave(nc.vector.tensor_copy, we_grp, we_raw, slice(0, WE_VECTOR_COLS))
        interleave(nc.scalar.copy, we_grp, we_raw, slice(WE_VECTOR_COLS, D))
        first_contraction(1, 0)
        first_contraction(0, 1)
        quantise_tokens(1, 1)
        first_contraction(1, 1)
        spread_ps = psum.tile([P, 2 * D], F32, tag="xt000")
        nc.tensor.matmul(out=spread_ps[:], lhsT=ones[:], rhs=free_rows[:], start=True, stop=True)
        nc.scalar.copy(out=spread[:], in_=spread_ps[:])

        add_b2(0)
        quantise(we_grp[:].rearrange("p n t -> p (n t)"), we_codes[:], we_scales[:])
        quantise_cat(0)
        second_contraction(0)
        add_b2(1)
        quantise_cat(1)
        second_contraction(1)
        for j in range(HALVES):
            add_be(j)
            measure(j)
        for j in range(HALVES):
            normed = keep.tile([P, D], F32, name="normed%d" % j)
            nc.vector.scalar_tensor_tensor(
                out=normed[:], in0=wave[:, j, :], scalar=inv_rms[j][:, 0:1], in1=g_all, op0=MULT, op1=MULT
            )
            nc.sync.dma_start(out=out_rows[:, j, :], in_=normed[:])
